import numpy as np
import ml_dtypes


BF16 = ml_dtypes.bfloat16


def bf(x):
    return np.asarray(x, np.float32).astype(BF16)


def f64(x):
    return np.asarray(x).astype(np.float64)


E2M1 = np.array([0.0, 0.5, 1.0, 1.5, 2.0, 3.0, 4.0, 6.0, -0.0, -0.5, -1.0, -1.5, -2.0, -3.0, -4.0, -6.0])


def pack_weight(w, fmt):
    k, n = w.shape
    w = f64(bf(w)).reshape(k // 32, 32, n)
    amax = np.abs(w).max(1)
    if fmt == "e4m3":
        byte = np.frexp(amax)[1] - 1 + 127 - 7
    else:
        mant, ex = np.frexp(amax / 6.0)
        byte = np.where(mant > 0.5, ex, ex - 1) + 127
    byte = np.clip(np.where(amax > 0, byte, 1), 1, 254)
    scaled = (w * np.exp2(127.0 - byte)[:, None, :]).reshape(k, n).astype(np.float32)
    by_word = np.ascontiguousarray(scaled.reshape(k // 512, 128, 4, n).transpose(0, 1, 3, 2))
    if fmt == "e4m3":
        words = by_word.astype(ml_dtypes.float8_e4m3fn).view(np.uint8)
    else:
        c = by_word.astype(ml_dtypes.float4_e2m1fn).view(np.uint8) & 0xF
        words = c[..., 0::2] | (c[..., 1::2] << 4)
    return np.ascontiguousarray(words), np.ascontiguousarray(byte.astype(np.uint8).reshape(k // 512, 16, n))


def unpack_weight(words, scales, fmt):
    g, p, n, _ = words.shape
    if fmt == "e4m3":
        vals = np.ascontiguousarray(words).view(ml_dtypes.float8_e4m3fn).astype(np.float64)
    else:
        nib = np.empty((g, p, n, 4), np.uint8)
        nib[..., 0::2] = words & 0xF
        nib[..., 1::2] = words >> 4
        vals = E2M1[nib]
    vals = vals * np.repeat(np.exp2(scales.astype(np.float64) - 127.0), 8, axis=1)[..., None]
    return vals.transpose(0, 1, 3, 2).reshape(g * 512, n)

def pack4(w):
    words, scales = pack_weight(w, "e2m1")
    return words.reshape(words.shape[0], 128, -1), scales


def unpack4(words, scales):
    return unpack_weight(words.reshape(words.shape[0], 128, -1, 2), scales, "e2m1")


def kspread(k):
    return np.exp2(np.repeat(np.random.randint(-6, 7, k // 32), 32).astype(np.float64))


B, T, D, NH, NG = 2, 256, 4096, 8, 4
GH = (D // NH) * NG
JIT = 0.06


def angles(t, d):
    i = np.arange(d // 2, dtype=np.float64)
    theta = (10000.0 ** (-(2.0 * (i - 1.0)))) / d
    return np.arange(t, dtype=np.float64)[:, None] * theta[None, :]


def rope(y, cos, sin):
    ye, yo = y[..., 0::2], y[..., 1::2]
    oe = ye * cos + yo * sin
    oo = -ye * sin + yo * cos
    return np.stack([oe, oo], axis=-1).reshape(y.shape)


def setup_inputs():
    s = kspread(D)
    aq = angles(T, D) + JIT * np.random.standard_normal((T, D // 2))
    ak = angles(T, GH) + JIT * np.random.standard_normal((T, GH // 2))
    x = np.random.standard_normal((B, T, D)) * s
    x_words, x_scales = pack4(x.reshape(B * T, D).T)
    Wq_words, Wq_scales = pack4(np.random.standard_normal((D, D)) / np.sqrt(D) / s[:, None])
    Wk_words, Wk_scales = pack4(np.random.standard_normal((D, GH)) / np.sqrt(D) / s[:, None])
    Wv_words, Wv_scales = pack4(np.random.standard_normal((D, GH)) / np.sqrt(D) / s[:, None])
    return {"x_words": x_words, "x_scales": x_scales,
            "Wq_words": Wq_words, "Wq_scales": Wq_scales,
            "Wk_words": Wk_words, "Wk_scales": Wk_scales,
            "Wv_words": Wv_words, "Wv_scales": Wv_scales,
            "cos_q": bf(np.cos(aq)), "sin_q": bf(np.sin(aq)),
            "cos_k": bf(np.cos(ak)), "sin_k": bf(np.sin(ak))}


def reference(x_words, x_scales, Wq_words, Wq_scales, Wk_words, Wk_scales, Wv_words, Wv_scales, cos_q, sin_q, cos_k, sin_k):
    xq = unpack4(x_words, x_scales).T.reshape(B, T, D)
    q = rope(xq @ unpack4(Wq_words, Wq_scales), f64(cos_q), f64(sin_q))
    k = rope(xq @ unpack4(Wk_words, Wk_scales), f64(cos_k), f64(sin_k))
    v = xq @ unpack4(Wv_words, Wv_scales)
    return q, k, v

@@ -1,0 +1,205 @@
+from contextlib import ExitStack
+
+import concourse.mybir as mybir
+
+F32 = mybir.dt.float32
+BF16 = mybir.dt.bfloat16
+U8 = mybir.dt.uint8
+I32 = mybir.dt.int32
+FP4X4 = mybir.dt.float4_e2m1fn_x4
+ALU = mybir.AluOpType
+
+P = 128
+PASSES = 8
+TOK_TILES = 4
+BLOCK = 512
+UNIT = 1024
+BLOCKS_PER_UNIT = UNIT // BLOCK
+PAIRS = BLOCK // 2
+N_BUF = 6
+WARM = 10
+TOGETHER = 6
+
+FLOPS = 2 * 512 * 4096 * 8192
+
+UNITS = (("q", 0), ("q", 1), ("k", 0), ("v", 0), ("q", 2), ("q", 3), ("k", 1), ("v", 1))
+
+
+def tile_selfattn_pa_kernel(
+    tc,
+    x_words, x_scales,
+    Wq_words, Wq_scales, Wk_words, Wk_scales, Wv_words, Wv_scales,
+    cos_q, sin_q, cos_k, sin_k,
+    out_0, out_1, out_2,
+):
+    nc = tc.nc
+    words = {"q": Wq_words, "k": Wk_words, "v": Wv_words}
+    scales = {"q": Wq_scales, "k": Wk_scales, "v": Wv_scales}
+    tables = {"q": (cos_q, sin_q), "k": (cos_k, sin_k)}
+    outs = {"q": out_0.flatten_outer_dims(), "k": out_1.flatten_outer_dims(), "v": out_2.flatten_outer_dims()}
+
+    with ExitStack() as ctx:
+        keep = ctx.enter_context(tc.tile_pool(name="keep", bufs=1))
+        work = ctx.enter_context(tc.tile_pool(name="work", bufs=3))
+        outp = ctx.enter_context(tc.tile_pool(name="outp", bufs=4))
+        psum = ctx.enter_context(tc.psum_pool(name="psum", bufs=8))
+        ctx.enter_context(tc.manual_schedule())
+
+        x_codes = keep.tile([P, PASSES, 2 * 512], U8, name="x_codes", align_bytes=256)
+        x_planes = keep.tile([P, PASSES, 512], U8, name="x_planes", align_bytes=256)
+        w_codes = []
+        w_planes = []
+        for i in range(N_BUF):
+            w_codes.append(keep.tile([P, PASSES, 2 * UNIT], U8, name="w_codes%d" % i, align_bytes=256))
+            w_planes.append(keep.tile([P, PASSES, UNIT], U8, name="w_planes%d" % i, align_bytes=256))
+        tabs = {}
+        for u, (kind, a) in enumerate(UNITS):
+            if kind != "v":
+                tabs[u] = keep.tile([P, 2, 2, UNIT // 2], BF16, name="tab%d" % u)
+        zero = keep.tile([P, BLOCK], BF16, name="zero")
+
+        def load_codes(dst, src, g0, g1, c0, c1, d0):
+            nc.sync.dma_start(
+                out=dst[:, g0:g1, d0 : d0 + c1 - c0].bitcast(I32),
+                in_=src[g0:g1, :, c0:c1].rearrange("g p c -> p g c").bitcast(I32),
+            )
+
+        def load_scales(dst, src, g0, g1, c0, c1):
+            for quad in range(4):
+                nc.sync.dma_start(
+                    out=dst[32 * quad : 32 * quad + 4, g0:g1, 0 : c1 - c0].bitcast(I32),
+                    in_=src[g0:g1, 4 * quad : 4 * quad + 4, c0:c1].rearrange("g r n -> r g n").bitcast(I32),
+                )
+
+        def load_tables(u):
+            kind, a = UNITS[u]
+            for cs in range(2):
+                nc.sync.dma_start(
+                    out=tabs[u][:, :, cs, :],
+                    in_=tables[kind][cs][:, a * (UNIT // 2) : (a + 1) * (UNIT // 2)].rearrange("(t p) i -> p t i", p=P),
+                )
+
+        def load_unit(u, by_block):
+            kind, a = UNITS[u]
+            buf = u % N_BUF
+            load_scales(w_planes[buf], scales[kind], 0, PASSES, a * UNIT, (a + 1) * UNIT)
+            if by_block:
+                for j in range(BLOCKS_PER_UNIT):
+                    c0 = 2 * (a * UNIT + j * BLOCK)
+                    load_codes(w_codes[buf], words[kind], 0, PASSES, c0, c0 + 2 * BLOCK, 2 * j * BLOCK)
+            else:
+                load_codes(w_codes[buf], words[kind], 0, PASSES, 2 * a * UNIT, 2 * (a + 1) * UNIT, 0)
+            if kind != "v":
+                load_tables(u)
+
+        nc.gpsimd.memset(zero[:], 0.0)
+        nc.vector.memset(x_planes[:, 0:2, :].bitcast(I32), 0)
+        nc.vector.memset(w_planes[0][:, 0:2, :].bitcast(I32), 0)
+        nc.vector.memset(x_planes[:, 2:PASSES, :].bitcast(I32), 0)
+        nc.vector.memset(w_planes[0][:, 2:PASSES, :].bitcast(I32), 0)
+        for i in range(1, N_BUF):
+            nc.vector.memset(w_planes[i][:].bitcast(I32), 0)
+
+        wq0 = words["q"]
+        load_codes(x_codes, x_words, 0, 1, 0, 1024, 0)
+        load_codes(w_codes[0], wq0, 0, 1, 0, 2 * UNIT, 0)
+        load_scales(x_planes, x_scales, 0, 2, 0, 512)
+        load_scales(w_planes[0], scales["q"], 0, 2, 0, UNIT)
+        load_codes(x_codes, x_words, 1, 2, 0, 1024, 0)
+        load_codes(w_codes[0], wq0, 1, 2, 0, 2 * UNIT, 0)
+        load_scales(x_planes, x_scales, 2, PASSES, 0, 512)
+        load_scales(w_planes[0], scales["q"], 2, PASSES, 0, UNIT)
+        load_codes(x_codes, x_words, 2, 4, 0, 1024, 0)
+        load_codes(w_codes[0], wq0, 2, 3, 0, 2 * UNIT, 0)
+        load_codes(w_codes[0], wq0, 3, 4, 0, 2 * UNIT, 0)
+        load_codes(x_codes, x_words, 4, PASSES, 0, 1024, 0)
+        for g in range(4, PASSES):
+            load_codes(w_codes[0], wq0, g, g + 1, 0, 2 * UNIT, 0)
+        load_tables(0)
+        load_unit(1, True)
+        for u in range(2, N_BUF):
+            load_unit(u, False)
+
+        warm = psum.tile([P, BLOCK], F32, name="acc")
+        for i in range(WARM):
+            nc.tensor.matmul(out=warm[:], lhsT=zero[:, 0:P], rhs=zero[:], start=True, stop=True)
+
+        def one_pass(acc, u, j, m, g):
+            buf = u % N_BUF
+            nc.tensor.matmul_mx(
+                out=acc[:],
+                lhsT=x_codes[:, g, 2 * P * m : 2 * P * (m + 1)].bitcast(FP4X4),
+                lhsT_scale=x_planes[:, g, P * m : P * (m + 1)],
+                rhs=w_codes[buf][:, g, 2 * BLOCK * j : 2 * BLOCK * (j + 1)].bitcast(FP4X4),
+                rhs_scale=w_planes[buf][:, g, BLOCK * j : BLOCK * (j + 1)],
+                start=(g == 0),
+                stop=(g == PASSES - 1),
+            )
+
+        waiting = []
+
+        def rope_back():
+            for t1, t2, dest in waiting:
+                res = outp.tile([P, BLOCK], F32, name="res")
+                nc.vector.tensor_tensor(
+                    out=res[:].rearrange("p (i e) -> p i e", e=2),
+                    in0=t1[:].rearrange("p (i e) -> p i e", e=2),
+                    in1=t2[:].rearrange("p e i -> p i e"),
+                    op=ALU.add,
+                )
+                nc.scalar.dma_start(out=dest, in_=res[:])
+            waiting.clear()
+
+        def epilogue(acc, u, j, m):
+            kind, a = UNITS[u]
+            col = a * UNIT + j * BLOCK
+            dest = outs[kind][m * P : (m + 1) * P, col : col + BLOCK]
+            if kind == "v":
+                rope_back()
+                res = outp.tile([P, BLOCK], F32, name="res")
+                nc.scalar.copy(out=res[:], in_=acc[:])
+                nc.scalar.dma_start(out=dest, in_=res[:])
+                return
+            cos = tabs[u][:, m % 2, 0, j * PAIRS : (j + 1) * PAIRS]
+            sin = tabs[u][:, m % 2, 1, j * PAIRS : (j + 1) * PAIRS]
+            halves = acc[:].rearrange("p (i e) -> p e i", e=2)
+            t1 = work.tile([P, BLOCK], F32, name="t1")
+            t2 = work.tile([P, 2, PAIRS], F32, name="t2")
+            nc.vector.tensor_tensor(
+                out=t1[:].rearrange("p (i e) -> p i e", e=2),
+                in0=acc[:].rearrange("p (i e) -> p i e", e=2),
+                in1=cos.unsqueeze(2).to_broadcast([P, PAIRS, 2]),
+                op=ALU.mult,
+            )
+            nc.vector.tensor_tensor(out=t2[:, 0, :], in0=halves[:, 1, :], in1=sin, op=ALU.mult)
+            nc.vector.scalar_tensor_tensor(
+                out=t2[:, 1, :], in0=halves[:, 0, :], scalar=-1.0, in1=sin, op0=ALU.mult, op1=ALU.mult
+            )
+            rope_back()
+            waiting.append((t1, t2, dest))
+
+        banks = []
+        for j in range(BLOCKS_PER_UNIT):
+            for m in range(TOK_TILES):
+                acc = psum.tile([P, BLOCK], F32, name="acc")
+                banks.append((acc, j, m))
+        for g in range(TOGETHER):
+            for acc, j, m in banks:
+                one_pass(acc, 0, j, m, g)
+        for acc, j, m in banks:
+            for g in range(TOGETHER, PASSES):
+                one_pass(acc, 0, j, m, g)
+        load_unit(N_BUF, False)
+        for acc, j, m in banks:
+            epilogue(acc, 0, j, m)
+
+        for u in range(1, len(UNITS)):
+            for j in range(BLOCKS_PER_UNIT):
+                for m in range(TOK_TILES):
+                    acc = psum.tile([P, BLOCK], F32, name="acc")
+                    for g in range(PASSES):
+                        one_pass(acc, u, j, m, g)
+                    epilogue(acc, u, j, m)
+            if u + N_BUF < len(UNITS):
+                load_unit(u + N_BUF, False)
+        rope_back()

@@ -19,10 +19,12 @@ PAIRS = BLOCK // 2
 N_BUF = 6
 WARM = 10
 TOGETHER = 6
+HALF = BLOCK // 2
 
 FLOPS = 2 * 512 * 4096 * 8192
 
 UNITS = (("q", 0), ("q", 1), ("k", 0), ("v", 0), ("q", 2), ("q", 3), ("k", 1), ("v", 1))
+LAST = (len(UNITS) - 1, BLOCKS_PER_UNIT - 1, TOK_TILES - 1)
 
 
 def tile_selfattn_pa_kernel(
@@ -40,8 +42,8 @@ def tile_selfattn_pa_kernel(
 
     with ExitStack() as ctx:
         keep = ctx.enter_context(tc.tile_pool(name="keep", bufs=1))
-        work = ctx.enter_context(tc.tile_pool(name="work", bufs=3))
-        outp = ctx.enter_context(tc.tile_pool(name="outp", bufs=4))
+        work = ctx.enter_context(tc.tile_pool(name="work", bufs=4))
+        outp = ctx.enter_context(tc.tile_pool(name="outp", bufs=8))
         psum = ctx.enter_context(tc.psum_pool(name="psum", bufs=8))
         ctx.enter_context(tc.manual_schedule())
 
@@ -65,7 +67,7 @@ def tile_selfattn_pa_kernel(
             )
 
         def load_scales(dst, src, g0, g1, c0, c1):
-            for quad in range(4):
+            for quad in (0, 2, 1, 3):
                 nc.sync.dma_start(
                     out=dst[32 * quad : 32 * quad + 4, g0:g1, 0 : c1 - c0].bitcast(I32),
                     in_=src[g0:g1, 4 * quad : 4 * quad + 4, c0:c1].rearrange("g r n -> r g n").bitcast(I32),
@@ -108,11 +110,12 @@ def tile_selfattn_pa_kernel(
         load_codes(x_codes, x_words, 1, 2, 0, 1024, 0)
         load_codes(w_codes[0], wq0, 1, 2, 0, 2 * UNIT, 0)
         load_scales(x_planes, x_scales, 2, PASSES, 0, 512)
-        load_scales(w_planes[0], scales["q"], 2, PASSES, 0, UNIT)
+        load_scales(w_planes[0], scales["q"], 2, 4, 0, UNIT)
         load_codes(x_codes, x_words, 2, 4, 0, 1024, 0)
         load_codes(w_codes[0], wq0, 2, 3, 0, 2 * UNIT, 0)
         load_codes(w_codes[0], wq0, 3, 4, 0, 2 * UNIT, 0)
         load_codes(x_codes, x_words, 4, PASSES, 0, 1024, 0)
+        load_scales(w_planes[0], scales["q"], 4, PASSES, 0, UNIT)
         for g in range(4, PASSES):
             load_codes(w_codes[0], wq0, g, g + 1, 0, 2 * UNIT, 0)
         load_tables(0)
@@ -124,14 +127,15 @@ def tile_selfattn_pa_kernel(
         for i in range(WARM):
             nc.tensor.matmul(out=warm[:], lhsT=zero[:, 0:P], rhs=zero[:], start=True, stop=True)
 
-        def one_pass(acc, u, j, m, g):
+        def one_pass(acc, u, j, m, g, c0=0, width=BLOCK):
             buf = u % N_BUF
+            lo = BLOCK * j + c0
             nc.tensor.matmul_mx(
                 out=acc[:],
                 lhsT=x_codes[:, g, 2 * P * m : 2 * P * (m + 1)].bitcast(FP4X4),
                 lhsT_scale=x_planes[:, g, P * m : P * (m + 1)],
-                rhs=w_codes[buf][:, g, 2 * BLOCK * j : 2 * BLOCK * (j + 1)].bitcast(FP4X4),
-                rhs_scale=w_planes[buf][:, g, BLOCK * j : BLOCK * (j + 1)],
+                rhs=w_codes[buf][:, g, 2 * lo : 2 * (lo + width)].bitcast(FP4X4),
+                rhs_scale=w_planes[buf][:, g, lo : lo + width],
                 start=(g == 0),
                 stop=(g == PASSES - 1),
             )
@@ -147,7 +151,7 @@ def tile_selfattn_pa_kernel(
                     in1=t2[:].rearrange("p e i -> p i e"),
                     op=ALU.add,
                 )
-                nc.scalar.dma_start(out=dest, in_=res[:])
+                nc.gpsimd.dma_start(out=dest, in_=res[:])
             waiting.clear()
 
         def epilogue(acc, u, j, m):
@@ -158,7 +162,10 @@ def tile_selfattn_pa_kernel(
                 rope_back()
                 res = outp.tile([P, BLOCK], F32, name="res")
                 nc.scalar.copy(out=res[:], in_=acc[:])
-                nc.scalar.dma_start(out=dest, in_=res[:])
+                if u == len(UNITS) - 1:
+                    nc.scalar.dma_start(out=dest, in_=res[:])
+                else:
+                    nc.gpsimd.dma_start(out=dest, in_=res[:])
                 return
             cos = tabs[u][:, m % 2, 0, j * PAIRS : (j + 1) * PAIRS]
             sin = tabs[u][:, m % 2, 1, j * PAIRS : (j + 1) * PAIRS]
@@ -196,6 +203,8 @@ def tile_selfattn_pa_kernel(
         for u in range(1, len(UNITS)):
             for j in range(BLOCKS_PER_UNIT):
                 for m in range(TOK_TILES):
+                    if (u, j, m) == LAST:
+                        continue
                     acc = psum.tile([P, BLOCK], F32, name="acc")
                     for g in range(PASSES):
                         one_pass(acc, u, j, m, g)
@@ -203,3 +212,19 @@ def tile_selfattn_pa_kernel(
             if u + N_BUF < len(UNITS):
                 load_unit(u + N_BUF, False)
         rope_back()
+
+        u, j, m = LAST
+        kind, a = UNITS[u]
+        for h in range(2):
+            acc = psum.tile([P, HALF], F32, name="acc")
+            for g in range(PASSES):
+                one_pass(acc, u, j, m, g, h * HALF, HALF)
+            col = a * UNIT + j * BLOCK + h * HALF
+            dest = outs[kind][m * P : (m + 1) * P, col : col + HALF]
+            res = outp.tile([P, HALF], F32, name="res")
+            if h == 0:
+                nc.vector.tensor_copy(out=res[:], in_=acc[:])
+                nc.sync.dma_start(out=dest, in_=res[:])
+            else:
+                nc.scalar.copy(out=res[:], in_=acc[:])
+                nc.scalar.dma_start(out=dest, in_=res[:])

@@ -44,6 +44,7 @@ def tile_selfattn_pa_kernel(
         keep = ctx.enter_context(tc.tile_pool(name="keep", bufs=1))
         work = ctx.enter_context(tc.tile_pool(name="work", bufs=4))
         outp = ctx.enter_context(tc.tile_pool(name="outp", bufs=8))
+        ypool = ctx.enter_context(tc.tile_pool(name="ypool", bufs=4))
         psum = ctx.enter_context(tc.psum_pool(name="psum", bufs=8))
         ctx.enter_context(tc.manual_schedule())
 
@@ -169,12 +170,14 @@ def tile_selfattn_pa_kernel(
                 return
             cos = tabs[u][:, m % 2, 0, j * PAIRS : (j + 1) * PAIRS]
             sin = tabs[u][:, m % 2, 1, j * PAIRS : (j + 1) * PAIRS]
-            halves = acc[:].rearrange("p (i e) -> p e i", e=2)
+            ysb = ypool.tile([P, BLOCK], F32, name="ysb")
+            nc.scalar.copy(out=ysb[:], in_=acc[:])
+            halves = ysb[:].rearrange("p (i e) -> p e i", e=2)
             t1 = work.tile([P, BLOCK], F32, name="t1")
             t2 = work.tile([P, 2, PAIRS], F32, name="t2")
             nc.vector.tensor_tensor(
                 out=t1[:].rearrange("p (i e) -> p i e", e=2),
-                in0=acc[:].rearrange("p (i e) -> p i e", e=2),
+                in0=ysb[:].rearrange("p (i e) -> p i e", e=2),
                 in1=cos.unsqueeze(2).to_broadcast([P, PAIRS, 2]),
                 op=ALU.mult,
             )

@@ -19,7 +19,7 @@ PAIRS = BLOCK // 2
 N_BUF = 6
 WARM = 10
 TOGETHER = 6
-HALF = BLOCK // 2
+LAST_PIECES = ((0, 256), (256, 128), (384, 128))
 
 FLOPS = 2 * 512 * 4096 * 8192
 
@@ -105,9 +105,10 @@ def tile_selfattn_pa_kernel(
 
         wq0 = words["q"]
         load_codes(x_codes, x_words, 0, 1, 0, 1024, 0)
-        load_codes(w_codes[0], wq0, 0, 1, 0, 2 * UNIT, 0)
+        load_codes(w_codes[0], wq0, 0, 1, 0, 2 * BLOCK, 0)
         load_scales(x_planes, x_scales, 0, 2, 0, 512)
         load_scales(w_planes[0], scales["q"], 0, 2, 0, UNIT)
+        load_codes(w_codes[0], wq0, 0, 1, 2 * BLOCK, 2 * UNIT, 2 * BLOCK)
         load_codes(x_codes, x_words, 1, 2, 0, 1024, 0)
         load_codes(w_codes[0], wq0, 1, 2, 0, 2 * UNIT, 0)
         load_scales(x_planes, x_scales, 2, PASSES, 0, 512)
@@ -218,14 +219,14 @@ def tile_selfattn_pa_kernel(
 
         u, j, m = LAST
         kind, a = UNITS[u]
-        for h in range(2):
-            acc = psum.tile([P, HALF], F32, name="acc")
+        for c0, width in LAST_PIECES:
+            acc = psum.tile([P, width], F32, name="acc")
             for g in range(PASSES):
-                one_pass(acc, u, j, m, g, h * HALF, HALF)
-            col = a * UNIT + j * BLOCK + h * HALF
-            dest = outs[kind][m * P : (m + 1) * P, col : col + HALF]
-            res = outp.tile([P, HALF], F32, name="res")
-            if h == 0:
+                one_pass(acc, u, j, m, g, c0, width)
+            col = a * UNIT + j * BLOCK + c0
+            dest = outs[kind][m * P : (m + 1) * P, col : col + width]
+            res = outp.tile([P, width], F32, name="res")
+            if c0 + width < BLOCK:
                 nc.vector.tensor_copy(out=res[:], in_=acc[:])
                 nc.sync.dma_start(out=dest, in_=res[:])
             else:

@@ -17,7 +17,7 @@ UNIT = 1024
 BLOCKS_PER_UNIT = UNIT // BLOCK
 PAIRS = BLOCK // 2
 N_BUF = 6
-WARM = 10
+WARM = 14
 TOGETHER = 6
 LAST_PIECES = ((0, 256), (256, 128), (384, 128))
 

@@ -96,9 +96,8 @@ def tile_selfattn_pa_kernel(
                 load_tables(u)
 
         nc.gpsimd.memset(zero[:], 0.0)
-        nc.vector.memset(x_planes[:, 0:2, :].bitcast(I32), 0)
+        nc.vector.memset(x_planes[:].bitcast(I32), 0)
         nc.vector.memset(w_planes[0][:, 0:2, :].bitcast(I32), 0)
-        nc.vector.memset(x_planes[:, 2:PASSES, :].bitcast(I32), 0)
         nc.vector.memset(w_planes[0][:, 2:PASSES, :].bitcast(I32), 0)
         for i in range(1, N_BUF):
             nc.vector.memset(w_planes[i][:].bitcast(I32), 0)
@@ -106,12 +105,11 @@ def tile_selfattn_pa_kernel(
         wq0 = words["q"]
         load_codes(x_codes, x_words, 0, 1, 0, 1024, 0)
         load_codes(w_codes[0], wq0, 0, 1, 0, 2 * BLOCK, 0)
-        load_scales(x_planes, x_scales, 0, 2, 0, 512)
+        load_scales(x_planes, x_scales, 0, PASSES, 0, 512)
         load_scales(w_planes[0], scales["q"], 0, 2, 0, UNIT)
         load_codes(w_codes[0], wq0, 0, 1, 2 * BLOCK, 2 * UNIT, 2 * BLOCK)
         load_codes(x_codes, x_words, 1, 2, 0, 1024, 0)
         load_codes(w_codes[0], wq0, 1, 2, 0, 2 * UNIT, 0)
-        load_scales(x_planes, x_scales, 2, PASSES, 0, 512)
         load_scales(w_planes[0], scales["q"], 2, 4, 0, UNIT)
         load_codes(x_codes, x_words, 2, 4, 0, 1024, 0)
         load_codes(w_codes[0], wq0, 2, 3, 0, 2 * UNIT, 0)

@@ -92,6 +92,8 @@ def tile_selfattn_pa_kernel(
                     load_codes(w_codes[buf], words[kind], 0, PASSES, c0, c0 + 2 * BLOCK, 2 * j * BLOCK)
             else:
                 load_codes(w_codes[buf], words[kind], 0, PASSES, 2 * a * UNIT, 2 * (a + 1) * UNIT, 0)
+            if u == 1:
+                load_tables(0)
             if kind != "v":
                 load_tables(u)
 
@@ -108,17 +110,15 @@ def tile_selfattn_pa_kernel(
         load_scales(x_planes, x_scales, 0, PASSES, 0, 512)
         load_scales(w_planes[0], scales["q"], 0, 2, 0, UNIT)
         load_codes(w_codes[0], wq0, 0, 1, 2 * BLOCK, 2 * UNIT, 2 * BLOCK)
-        load_codes(x_codes, x_words, 1, 2, 0, 1024, 0)
+        load_codes(x_codes, x_words, 1, 3, 0, 1024, 0)
         load_codes(w_codes[0], wq0, 1, 2, 0, 2 * UNIT, 0)
         load_scales(w_planes[0], scales["q"], 2, 4, 0, UNIT)
-        load_codes(x_codes, x_words, 2, 4, 0, 1024, 0)
         load_codes(w_codes[0], wq0, 2, 3, 0, 2 * UNIT, 0)
         load_codes(w_codes[0], wq0, 3, 4, 0, 2 * UNIT, 0)
-        load_codes(x_codes, x_words, 4, PASSES, 0, 1024, 0)
+        load_codes(x_codes, x_words, 3, PASSES, 0, 1024, 0)
         load_scales(w_planes[0], scales["q"], 4, PASSES, 0, UNIT)
         for g in range(4, PASSES):
             load_codes(w_codes[0], wq0, g, g + 1, 0, 2 * UNIT, 0)
-        load_tables(0)
         load_unit(1, True)
         for u in range(2, N_BUF):
             load_unit(u, False)

@@ -112,8 +112,8 @@ def tile_selfattn_pa_kernel(
         load_codes(w_codes[0], wq0, 0, 1, 2 * BLOCK, 2 * UNIT, 2 * BLOCK)
         load_codes(x_codes, x_words, 1, 3, 0, 1024, 0)
         load_codes(w_codes[0], wq0, 1, 2, 0, 2 * UNIT, 0)
-        load_scales(w_planes[0], scales["q"], 2, 4, 0, UNIT)
         load_codes(w_codes[0], wq0, 2, 3, 0, 2 * UNIT, 0)
+        load_scales(w_planes[0], scales["q"], 2, 4, 0, UNIT)
         load_codes(w_codes[0], wq0, 3, 4, 0, 2 * UNIT, 0)
         load_codes(x_codes, x_words, 3, PASSES, 0, 1024, 0)
         load_scales(w_planes[0], scales["q"], 4, PASSES, 0, UNIT)

from contextlib import ExitStack

import concourse.mybir as mybir

F32 = mybir.dt.float32
BF16 = mybir.dt.bfloat16
U8 = mybir.dt.uint8
I32 = mybir.dt.int32
FP4X4 = mybir.dt.float4_e2m1fn_x4
ALU = mybir.AluOpType

P = 128
PASSES = 8
TOK_TILES = 4
BLOCK = 512
UNIT = 1024
BLOCKS_PER_UNIT = UNIT // BLOCK
PAIRS = BLOCK // 2
N_BUF = 6
WARM = 14
TOGETHER = 6
LAST_PIECES = ((0, 256), (256, 128), (384, 128))

FLOPS = 2 * 512 * 4096 * 8192

UNITS = (("q", 0), ("q", 1), ("k", 0), ("v", 0), ("q", 2), ("q", 3), ("k", 1), ("v", 1))
LAST = (len(UNITS) - 1, BLOCKS_PER_UNIT - 1, TOK_TILES - 1)


def tile_selfattn_pa_kernel(
    tc,
    x_words, x_scales,
    Wq_words, Wq_scales, Wk_words, Wk_scales, Wv_words, Wv_scales,
    cos_q, sin_q, cos_k, sin_k,
    out_0, out_1, out_2,
):
    nc = tc.nc
    words = {"q": Wq_words, "k": Wk_words, "v": Wv_words}
    scales = {"q": Wq_scales, "k": Wk_scales, "v": Wv_scales}
    tables = {"q": (cos_q, sin_q), "k": (cos_k, sin_k)}
    outs = {"q": out_0.flatten_outer_dims(), "k": out_1.flatten_outer_dims(), "v": out_2.flatten_outer_dims()}

    with ExitStack() as ctx:
        keep = ctx.enter_context(tc.tile_pool(name="keep", bufs=1))
        work = ctx.enter_context(tc.tile_pool(name="work", bufs=4))
        outp = ctx.enter_context(tc.tile_pool(name="outp", bufs=8))
        ypool = ctx.enter_context(tc.tile_pool(name="ypool", bufs=4))
        psum = ctx.enter_context(tc.psum_pool(name="psum", bufs=8))
        ctx.enter_context(tc.manual_schedule())

        x_codes = keep.tile([P, PASSES, 2 * 512], U8, name="x_codes", align_bytes=256)
        x_planes = keep.tile([P, PASSES, 512], U8, name="x_planes", align_bytes=256)
        w_codes = []
        w_planes = []
        for i in range(N_BUF):
            w_codes.append(keep.tile([P, PASSES, 2 * UNIT], U8, name="w_codes%d" % i, align_bytes=256))
            w_planes.append(keep.tile([P, PASSES, UNIT], U8, name="w_planes%d" % i, align_bytes=256))
        tabs = {}
        for u, (kind, a) in enumerate(UNITS):
            if kind != "v":
                tabs[u] = keep.tile([P, 2, 2, UNIT // 2], BF16, name="tab%d" % u)
        zero = keep.tile([P, BLOCK], BF16, name="zero")

        def load_codes(dst, src, g0, g1, c0, c1, d0):
            nc.sync.dma_start(
                out=dst[:, g0:g1, d0 : d0 + c1 - c0].bitcast(I32),
                in_=src[g0:g1, :, c0:c1].rearrange("g p c -> p g c").bitcast(I32),
            )

        def load_scales(dst, src, g0, g1, c0, c1):
            for quad in (0, 2, 1, 3):
                nc.sync.dma_start(
                    out=dst[32 * quad : 32 * quad + 4, g0:g1, 0 : c1 - c0].bitcast(I32),
                    in_=src[g0:g1, 4 * quad : 4 * quad + 4, c0:c1].rearrange("g r n -> r g n").bitcast(I32),
                )

        def load_tables(u):
            kind, a = UNITS[u]
            for cs in range(2):
                nc.sync.dma_start(
                    out=tabs[u][:, :, cs, :],
                    in_=tables[kind][cs][:, a * (UNIT // 2) : (a + 1) * (UNIT // 2)].rearrange("(t p) i -> p t i", p=P),
                )

        def load_unit(u, by_block):
            kind, a = UNITS[u]
            buf = u % N_BUF
            load_scales(w_planes[buf], scales[kind], 0, PASSES, a * UNIT, (a + 1) * UNIT)
            if by_block:
                for j in range(BLOCKS_PER_UNIT):
                    c0 = 2 * (a * UNIT + j * BLOCK)
                    load_codes(w_codes[buf], words[kind], 0, PASSES, c0, c0 + 2 * BLOCK, 2 * j * BLOCK)
            else:
                load_codes(w_codes[buf], words[kind], 0, PASSES, 2 * a * UNIT, 2 * (a + 1) * UNIT, 0)
            if u == 1:
                load_tables(0)
            if kind != "v":
                load_tables(u)

        nc.gpsimd.memset(zero[:], 0.0)
        nc.vector.memset(x_planes[:].bitcast(I32), 0)
        nc.vector.memset(w_planes[0][:, 0:2, :].bitcast(I32), 0)
        nc.vector.memset(w_planes[0][:, 2:PASSES, :].bitcast(I32), 0)
        for i in range(1, N_BUF):
            nc.vector.memset(w_planes[i][:].bitcast(I32), 0)

        wq0 = words["q"]
        load_codes(x_codes, x_words, 0, 1, 0, 1024, 0)
        load_codes(w_codes[0], wq0, 0, 1, 0, 2 * BLOCK, 0)
        load_scales(x_planes, x_scales, 0, PASSES, 0, 512)
        load_scales(w_planes[0], scales["q"], 0, 2, 0, UNIT)
        load_codes(w_codes[0], wq0, 0, 1, 2 * BLOCK, 2 * UNIT, 2 * BLOCK)
        load_codes(x_codes, x_words, 1, 3, 0, 1024, 0)
        load_codes(w_codes[0], wq0, 1, 2, 0, 2 * UNIT, 0)
        load_codes(w_codes[0], wq0, 2, 3, 0, 2 * UNIT, 0)
        load_scales(w_planes[0], scales["q"], 2, 4, 0, UNIT)
        load_codes(w_codes[0], wq0, 3, 4, 0, 2 * UNIT, 0)
        load_codes(x_codes, x_words, 3, PASSES, 0, 1024, 0)
        load_scales(w_planes[0], scales["q"], 4, PASSES, 0, UNIT)
        for g in range(4, PASSES):
            load_codes(w_codes[0], wq0, g, g + 1, 0, 2 * UNIT, 0)
        load_unit(1, True)
        for u in range(2, N_BUF):
            load_unit(u, False)

        warm = psum.tile([P, BLOCK], F32, name="acc")
        for i in range(WARM):
            nc.tensor.matmul(out=warm[:], lhsT=zero[:, 0:P], rhs=zero[:], start=True, stop=True)

        def one_pass(acc, u, j, m, g, c0=0, width=BLOCK):
            buf = u % N_BUF
            lo = BLOCK * j + c0
            nc.tensor.matmul_mx(
                out=acc[:],
                lhsT=x_codes[:, g, 2 * P * m : 2 * P * (m + 1)].bitcast(FP4X4),
                lhsT_scale=x_planes[:, g, P * m : P * (m + 1)],
                rhs=w_codes[buf][:, g, 2 * lo : 2 * (lo + width)].bitcast(FP4X4),
                rhs_scale=w_planes[buf][:, g, lo : lo + width],
                start=(g == 0),
                stop=(g == PASSES - 1),
            )

        waiting = []

        def rope_back():
            for t1, t2, dest in waiting:
                res = outp.tile([P, BLOCK], F32, name="res")
                nc.vector.tensor_tensor(
                    out=res[:].rearrange("p (i e) -> p i e", e=2),
                    in0=t1[:].rearrange("p (i e) -> p i e", e=2),
                    in1=t2[:].rearrange("p e i -> p i e"),
                    op=ALU.add,
                )
                nc.gpsimd.dma_start(out=dest, in_=res[:])
            waiting.clear()

        def epilogue(acc, u, j, m):
            kind, a = UNITS[u]
            col = a * UNIT + j * BLOCK
            dest = outs[kind][m * P : (m + 1) * P, col : col + BLOCK]
            if kind == "v":
                rope_back()
                res = outp.tile([P, BLOCK], F32, name="res")
                nc.scalar.copy(out=res[:], in_=acc[:])
                if u == len(UNITS) - 1:
                    nc.scalar.dma_start(out=dest, in_=res[:])
                else:
                    nc.gpsimd.dma_start(out=dest, in_=res[:])
                return
            cos = tabs[u][:, m % 2, 0, j * PAIRS : (j + 1) * PAIRS]
            sin = tabs[u][:, m % 2, 1, j * PAIRS : (j + 1) * PAIRS]
            ysb = ypool.tile([P, BLOCK], F32, name="ysb")
            nc.scalar.copy(out=ysb[:], in_=acc[:])
            halves = ysb[:].rearrange("p (i e) -> p e i", e=2)
            t1 = work.tile([P, BLOCK], F32, name="t1")
            t2 = work.tile([P, 2, PAIRS], F32, name="t2")
            nc.vector.tensor_tensor(
                out=t1[:].rearrange("p (i e) -> p i e", e=2),
                in0=ysb[:].rearrange("p (i e) -> p i e", e=2),
                in1=cos.unsqueeze(2).to_broadcast([P, PAIRS, 2]),
                op=ALU.mult,
            )
            nc.vector.tensor_tensor(out=t2[:, 0, :], in0=halves[:, 1, :], in1=sin, op=ALU.mult)
            nc.vector.scalar_tensor_tensor(
                out=t2[:, 1, :], in0=halves[:, 0, :], scalar=-1.0, in1=sin, op0=ALU.mult, op1=ALU.mult
            )
            rope_back()
            waiting.append((t1, t2, dest))

        banks = []
        for j in range(BLOCKS_PER_UNIT):
            for m in range(TOK_TILES):
                acc = psum.tile([P, BLOCK], F32, name="acc")
                banks.append((acc, j, m))
        for g in range(TOGETHER):
            for acc, j, m in banks:
                one_pass(acc, 0, j, m, g)
        for acc, j, m in banks:
            for g in range(TOGETHER, PASSES):
                one_pass(acc, 0, j, m, g)
        load_unit(N_BUF, False)
        for acc, j, m in banks:
            epilogue(acc, 0, j, m)

        for u in range(1, len(UNITS)):
            for j in range(BLOCKS_PER_UNIT):
                for m in range(TOK_TILES):
                    if (u, j, m) == LAST:
                        continue
                    acc = psum.tile([P, BLOCK], F32, name="acc")
                    for g in range(PASSES):
                        one_pass(acc, u, j, m, g)
                    epilogue(acc, u, j, m)
            if u + N_BUF < len(UNITS):
                load_unit(u + N_BUF, False)
        rope_back()

        u, j, m = LAST
        kind, a = UNITS[u]
        for c0, width in LAST_PIECES:
            acc = psum.tile([P, width], F32, name="acc")
            for g in range(PASSES):
                one_pass(acc, u, j, m, g, c0, width)
            col = a * UNIT + j * BLOCK + c0
            dest = outs[kind][m * P : (m + 1) * P, col : col + width]
            res = outp.tile([P, width], F32, name="res")
            if c0 + width < BLOCK:
                nc.vector.tensor_copy(out=res[:], in_=acc[:])
                nc.sync.dma_start(out=dest, in_=res[:])
            else:
                nc.scalar.copy(out=res[:], in_=acc[:])
                nc.scalar.dma_start(out=dest, in_=res[:])
